import numpy as np
import ml_dtypes


def mxq(x, axis, fmt="e4m3"):
    dtype, down = {"e4m3": (ml_dtypes.float8_e4m3fn, 7), "e5m2": (ml_dtypes.float8_e5m2, 14)}[fmt]
    v = np.moveaxis(np.asarray(x, np.float32).astype(ml_dtypes.bfloat16).astype(np.float64), axis, -1)
    blocks = v.reshape(v.shape[:-1] + (-1, 32))
    amax = np.abs(blocks).max(-1, keepdims=True)
    byte = np.maximum(np.where(amax > 0, np.frexp(amax)[1] - 1 + 127, 0) - down, 1)
    scale = np.exp2(byte - 127.0)
    codes = (blocks / scale).astype(np.float32).astype(dtype).astype(np.float64)
    return np.moveaxis((codes * scale).reshape(v.shape), -1, axis)


WIDE = False


def mx_kscale(k):
    if not WIDE:
        return np.ones(k)
    levels = np.array([10, -10, 5, -5, 0])
    if k % 512:
        return np.exp2(np.random.permutation(np.resize(levels, k // 32))).repeat(32)
    a = np.empty((k // 512, 16))
    for p in range(k // 512):
        a[p, :8] = np.random.permutation(np.resize(levels, 8))
        for g in range(8):
            far = levels[np.abs(levels - a[p, g]) >= 10]
            a[p, g + 8] = far[np.random.randint(len(far))]
    return np.exp2(a.ravel()).repeat(32)


BF16 = ml_dtypes.bfloat16


def bf(x):
    return np.asarray(x, np.float32).astype(BF16)


def f64(x):
    return np.asarray(x).astype(np.float64)


B, H, W, CH, NC, DIM = 4, 16, 16, 512, 22, 512


def _patches3x3(a):
    b, h, w, c = a.shape
    p = np.pad(a, ((0, 0), (1, 1), (1, 1), (0, 0)))
    return np.stack([p[:, i:i + h, j:j + w, :] for i in range(3) for j in range(3)], axis=3)


def setup_inputs():
    s = mx_kscale(CH)
    lim = np.sqrt(6.0 / (CH * 9))
    return {"x": bf(np.random.standard_normal((B, H, W, CH)) * s),
            "seg_mask": bf(np.random.random((B, H, W, NC)) * (np.random.random((B, H, W, NC)) > 0.25)),
            "conv_w": bf(np.random.uniform(-lim, lim, (CH, 3, 3, DIM)) / s[:, None, None, None])}


def reference(x, seg_mask, conv_w):
    x, seg_mask, conv_w = f64(x), f64(seg_mask), f64(conv_w)
    s_patch = _patches3x3(seg_mask)
    m = seg_mask[:, :, :, None, :]
    s_max = np.max(m, axis=-1, keepdims=True)
    sel = np.sum(np.where(m == s_max, s_patch, 0.0), axis=-1)
    cnt = np.sum((sel != 0.0).astype(np.float64), axis=-1, keepdims=True)
    norm = np.where(cnt > 0, 9.0 / np.maximum(cnt, 1.0), 0.0)
    xp = _patches3x3(x)
    xp = xp * sel[..., None]
    w = conv_w.reshape(CH, 9, DIM)
    xq = mxq(xp.reshape(B * H * W, 9 * CH), 1, "e4m3")
    wq = mxq(w.transpose(1, 0, 2).reshape(9 * CH, DIM), 0, "e4m3")
    out = (xq @ wq).reshape(B, H, W, DIM) * norm
    return out

@@ -1,0 +1,304 @@
+from contextlib import ExitStack
+
+import concourse.mybir as mybir
+from concourse.masks import make_identity
+
+F32 = mybir.dt.float32
+BF16 = mybir.dt.bfloat16
+U32 = mybir.dt.uint32
+U8 = mybir.dt.uint8
+FP8X4 = mybir.dt.float8_e4m3fn_x4
+ALU = mybir.AluOpType
+ACTF = mybir.ActivationFunctionType
+AX = mybir.AxisListType
+
+P = 128
+NCLS = 22
+TAPS = 9
+DIM = 512
+CH = 512
+PIX = 256
+FLOPS = 2 * 1024 * 4608 * 512
+
+PHASES = ((0, 1), (2, 3))
+W_ON_VECTOR = (2, 5, 8)
+S_HEAD = (0, 1)
+S_FILL = (3, 4, 6, 7)
+FILL = (2, 4, 6, 8, 10, 12, 14, 16)
+WPARTS = 4
+WARM0 = 6
+LAG = 2
+
+
+def tile_partialconvolution_kernel(tc, x, seg_mask, conv_w, out):
+    nc = tc.nc
+    xv = x.rearrange("b h w c -> (b h w) c").rearrange("(m p) c -> p m c", p=P)
+    sv = seg_mask.rearrange("b h w c -> (b h w) c").rearrange("(m p) c -> p m c", p=P)
+    wv = conv_w.rearrange("(p t) i j d -> p t (i j) d", t=4)
+    ov = out.rearrange("b h w d -> (b h w) d")
+
+    with ExitStack() as ctx:
+        ctx.enter_context(tc.manual_schedule())
+        const = ctx.enter_context(tc.tile_pool(name="const", bufs=1))
+        gpool = ctx.enter_context(tc.tile_pool(name="gated", bufs=16))
+        xqpool = ctx.enter_context(tc.tile_pool(name="xquant", bufs=8))
+        rpool = ctx.enter_context(tc.tile_pool(name="result", bufs=4))
+        psum = ctx.enter_context(tc.psum_pool(name="psum", bufs=4))
+
+        m0 = const.tile([P, 8, NCLS], BF16, name="m0")
+        xs = [const.tile([P, 4, CH], BF16, name="xs%d" % ip) for ip in range(2)]
+        wraw = [const.tile([P, 4, DIM], BF16, name="wraw%d" % k) for k in range(TAPS)]
+
+        def load_w(k):
+            nc.sync.dma_start(out=wraw[k][:], in_=wv[:, :, k, :])
+
+        def load_x(ip):
+            nc.sync.dma_start(out=xs[ip][:], in_=xv[:, 4 * ip : 4 * ip + 4, :])
+
+        nc.sync.dma_start(out=m0[:], in_=sv)
+        load_w(0)
+        load_x(0)
+        for k in range(1, 4):
+            load_w(k)
+        load_x(1)
+        for k in range(4, TAPS):
+            load_w(k)
+
+        zeros = const.tile([P, DIM], BF16, name="zeros")
+        nc.vector.memset(zeros[:], 0.0)
+
+        def warm(dst, times, width=DIM):
+            for i in range(times):
+                nc.tensor.matmul(out=dst, lhsT=zeros[:, 0:P], rhs=zeros[:, 0:width], start=True, stop=True)
+
+        warmt = psum.tile([P, DIM], F32, name="warmt", tag="tp")
+        warm(warmt[:], WARM0)
+        ident = const.tile([P, P], F32, name="ident")
+        make_identity(nc, ident[:])
+        wide = const.tile([P, 3, 384], BF16, name="wide")
+        nc.vector.memset(wide[:], 0.0)
+        nc.vector.tensor_copy(out=wide[:, :, 128:256], in_=ident[:].unsqueeze(1).to_broadcast([P, 3, P]))
+        w16 = wide[:, :, 128:256].rearrange("p j (a b) -> p j a b", b=16)
+        nc.vector.memset(w16[:, 0, :, 0:1], 0.0)
+        nc.vector.memset(w16[:, 2, :, 15:16], 0.0)
+        gq = [const.tile([P, 2, 4 * PIX], BF16, name="gq%d" % k, align_bytes=64) for k in range(TAPS)]
+        shift = [16 * (k // 3 - 1) + k % 3 - 1 for k in range(TAPS)]
+        for k in range(TAPS):
+            if shift[k] < 0:
+                nc.gpsimd.memset(gq[k][:, :, 0 : -4 * shift[k]], 0.0)
+            if shift[k] > 0:
+                nc.gpsimd.memset(gq[k][:, :, 4 * (PIX - shift[k]) : 4 * PIX], 0.0)
+
+        mx0 = const.tile([P, 8], F32, name="mx0")
+        e0 = const.tile([P, 8, NCLS], BF16, name="e0")
+        prod = const.tile([P, 2, TAPS, 4, NCLS], BF16, name="prod")
+        sels = const.tile([P, 2, TAPS, 4], F32, name="sels")
+        nz = const.tile([P, 2, TAPS, 4], BF16, name="nz")
+        cmax = const.tile([P, 8], F32, name="cmax")
+        crec = const.tile([P, 8], F32, name="crec")
+        norm = const.tile([P, 8], F32, name="norm")
+
+        nc.vector.tensor_reduce(out=mx0[:], in_=m0[:], axis=AX.X, op=ALU.max)
+        nc.vector.tensor_tensor(
+            out=e0[:], in0=m0[:], in1=mx0[:].unsqueeze(2).to_broadcast([P, 8, NCLS]), op=ALU.is_equal
+        )
+
+        def shift_onehot(tg):
+            esh = psum.tile([P, 3, 8, NCLS], BF16, name="esh", tag="acc")
+            di = tg - 1
+            for kk in range(3):
+                sh = 16 * di + kk - 1
+                nc.tensor.matmul(
+                    out=esh[:, kk, :, :],
+                    lhsT=wide[:, kk, 128 - sh : 256 - sh],
+                    rhs=e0[:],
+                    start=True,
+                    stop=(di == 0),
+                )
+                if di == 1:
+                    nc.tensor.matmul(
+                        out=esh[:, kk, 1:8:2, :],
+                        lhsT=wide[:, kk, 256 - sh : 384 - sh],
+                        rhs=e0[:, 0:8:2, :],
+                        start=False,
+                        stop=True,
+                    )
+                if di == -1:
+                    nc.tensor.matmul(
+                        out=esh[:, kk, 0:8:2, :],
+                        lhsT=wide[:, kk, -sh : 128 - sh],
+                        rhs=e0[:, 1:8:2, :],
+                        start=False,
+                        stop=True,
+                    )
+            return esh
+
+        def dot_classes(ip, tg, esh):
+            ks = slice(3 * tg, 3 * tg + 3)
+            nc.vector.tensor_tensor(
+                out=prod[:, ip, ks, :, :],
+                in0=esh[:, :, 4 * ip : 4 * ip + 4, :],
+                in1=m0[:, 4 * ip : 4 * ip + 4, :].unsqueeze(1).to_broadcast([P, 3, 4, NCLS]),
+                op=ALU.mult,
+            )
+            nc.vector.tensor_reduce(out=sels[:, ip, ks, :], in_=prod[:, ip, ks, :, :], axis=AX.X, op=ALU.add)
+
+        def count_taps():
+            nc.vector.tensor_single_scalar(out=nz[:], in_=sels[:], scalar=0.0, op=ALU.not_equal)
+            cp = psum.tile([P, 2, 4], F32, name="cp", tag="acc")
+            steps = []
+            for k in range(TAPS):
+                sh = shift[k]
+                steps.append((cp[:, :, :], 128 + sh, nz[:, :, k, :]))
+                if k >= 6:
+                    steps.append((cp[:, :, 0:4:2], sh, nz[:, :, k, 1:4:2]))
+                if k < 3:
+                    steps.append((cp[:, :, 1:4:2], 256 + sh, nz[:, :, k, 0:4:2]))
+            for i, (o, c0, r) in enumerate(steps):
+                nc.tensor.matmul(
+                    out=o, lhsT=wide[:, 1, c0 : c0 + P], rhs=r, start=(i == 0), stop=(i == len(steps) - 1)
+                )
+            return cp
+
+        def make_norm(cp):
+            nc.vector.tensor_scalar_max(out=cmax[:], in0=cp[:].rearrange("p a b -> p (a b)"), scalar1=1.0)
+            nc.vector.reciprocal(out=crec[:], in_=cmax[:])
+            nc.vector.tensor_scalar_mul(out=norm[:], in0=crec[:], scalar1=9.0)
+
+        wq = const.tile([P, TAPS, DIM], U32, name="wq", align_bytes=64)
+        ws = const.tile([P, TAPS, DIM], U8, name="ws", align_bytes=64)
+        wg = [const.tile([P, DIM, 4], BF16, name="wg%d" % k, align_bytes=64) for k in range(TAPS)]
+
+        def regroup_w(k, part, parts):
+            n = DIM // parts
+            dst = wg[k][:, part * n : (part + 1) * n, :].rearrange("p (c i) t -> p c t i", i=4)
+            src = wraw[k][:, :, part * n : (part + 1) * n].rearrange("p t (c i) -> p c t i", i=4)
+            if k in W_ON_VECTOR:
+                nc.vector.tensor_copy(out=dst, in_=src)
+            else:
+                nc.scalar.copy(out=dst, in_=src)
+
+        def quantise_w(k):
+            if k in W_ON_VECTOR:
+                regroup_w(k, 0, 1)
+            nc.vector.quantize_mx(
+                out=wq[:, k, :].bitcast(FP8X4), scales=ws[:, k, :], in_=wg[k][:].rearrange("p d t -> p (d t)")
+            )
+
+        xr = [const.tile([P, 4, CH], BF16, name="xr%d" % ip) for ip in range(2)]
+
+        def reorder_x(ip):
+            for m in range(4):
+                nc.vector.tensor_copy(
+                    out=xr[ip][:, m, :].bitcast(F32).rearrange("p (u w) -> p u w", u=2),
+                    in_=xs[ip][:, m, :].bitcast(F32).rearrange("p (w u) -> p u w", u=2),
+                )
+
+        gts = {}
+        psts = {}
+        xq = {}
+        xsc = {}
+        acc = {}
+
+        def gate(b, k):
+            for mm in range(2):
+                m = 2 * b + mm
+                gt = gpool.tile([P, CH], BF16, name="gt", tag="gt")
+                nc.vector.tensor_scalar_mul(
+                    out=gt[:], in0=xr[m // 4][:, m % 4, :], scalar1=sels[:, m // 4, k, m % 4 : m % 4 + 1]
+                )
+                gts[(b, k, mm)] = gt
+
+        def transpose(b, k):
+            pst = psum.tile([P, 2, PIX], F32, name="pst", tag="tp")
+            for mm in range(2):
+                words = gts[(b, k, mm)][:].bitcast(F32)
+                for u in range(2):
+                    nc.tensor.transpose(
+                        out=pst[:, u, mm * P : (mm + 1) * P], in_=words[:, u * P : (u + 1) * P], identity=ident[:]
+                    )
+            psts[(b, k)] = pst
+
+        def evacuate(b, k):
+            sh = shift[k]
+            d0, d1 = max(0, -sh), min(PIX, PIX - sh)
+            nc.scalar.copy(
+                out=gq[k][:, b % 2, 4 * d0 : 4 * d1].bitcast(F32).rearrange("p (x u) -> p x u", u=2),
+                in_=psts[(b, k)][:, :, d0 + sh : d1 + sh].rearrange("p u x -> p x u"),
+            )
+
+        def quantise_x(b, k):
+            xq[(b, k)] = xqpool.tile([P, PIX], U32, name="xq", tag="xq", align_bytes=64)
+            xsc[(b, k)] = xqpool.tile([P, PIX], U8, name="xsc", tag="xsc", align_bytes=64)
+            nc.vector.quantize_mx(
+                out=xq[(b, k)][:].bitcast(FP8X4), scales=xsc[(b, k)][:], in_=gq[k][:, b % 2, :]
+            )
+
+        def multiply(b, k):
+            for mm in range(2):
+                if k == 0:
+                    acc[(b, mm)] = psum.tile([P, DIM], F32, name="acc", tag="acc")
+                nc.tensor.matmul_mx(
+                    out=acc[(b, mm)][:],
+                    lhsT=xq[(b, k)][:, mm * P : (mm + 1) * P].bitcast(FP8X4),
+                    lhsT_scale=xsc[(b, k)][:, mm * P : (mm + 1) * P],
+                    rhs=wq[:, k, :].bitcast(FP8X4),
+                    rhs_scale=ws[:, k, :],
+                    start=(k == 0),
+                    stop=(k == TAPS - 1),
+                )
+                if k == TAPS - 1:
+                    m = 2 * b + mm
+                    res = rpool.tile([P, DIM], F32, name="res", tag="res")
+                    nc.scalar.activation(out=res[:], in_=acc[(b, mm)][:], func=ACTF.Copy, scale=norm[:, m : m + 1])
+                    nc.sync.dma_start(out=ov[m * P : (m + 1) * P, :], in_=res[:])
+
+        esh = [shift_onehot(tg) for tg in range(3)]
+        for k in S_HEAD:
+            for part in range(WPARTS):
+                regroup_w(k, part, WPARTS)
+        sfill = [(k, part) for k in S_FILL for part in range(WPARTS)]
+        for tg in range(3):
+            dot_classes(0, tg, esh[tg])
+        reorder_x(0)
+
+        steps = [(ph, k) for ph in range(len(PHASES)) for k in range(TAPS)]
+
+        def front(j):
+            ph, k = steps[j]
+            for b in PHASES[ph]:
+                gate(b, k)
+
+        def middle(j):
+            ph, k = steps[j]
+            for b in PHASES[ph]:
+                transpose(b, k)
+            for b in PHASES[ph]:
+                evacuate(b, k)
+            for f in sfill[(FILL[j - 1] if 0 < j <= len(FILL) else 0 if j == 0 else 99) : (FILL[j] if j < len(FILL) else 99)]:
+                regroup_w(f[0], f[1], WPARTS)
+
+        def back(j):
+            ph, k = steps[j]
+            for b in PHASES[ph]:
+                multiply(b, k)
+
+        for j in range(LAG):
+            front(j)
+        for tg in range(3):
+            dot_classes(1, tg, esh[tg])
+        cp = count_taps()
+        for j in range(LAG):
+            middle(j)
+        make_norm(cp)
+        reorder_x(1)
+        for j in range(len(steps)):
+            if j + LAG < len(steps):
+                front(j + LAG)
+                middle(j + LAG)
+            ph, k = steps[j]
+            for b in PHASES[ph]:
+                quantise_x(b, k)
+            if ph == 0:
+                quantise_w(k)
+            back(j)

@@ -20,14 +20,19 @@ CH = 512
 PIX = 256
 FLOPS = 2 * 1024 * 4608 * 512
 
-PHASES = ((0, 1), (2, 3))
-W_ON_VECTOR = (2, 5, 8)
-S_HEAD = (0, 1)
-S_FILL = (3, 4, 6, 7)
-FILL = (2, 4, 6, 8, 10, 12, 14, 16)
+ORDER = (4, 3, 5, 0, 1, 2, 6, 7, 8)
+V_PARTS = (0, 4, 1, 1, 1, 1, 1, 1, 1)
+HEAD_PARTS = 4
+CHUNK_PARTS = 2
 WPARTS = 4
-WARM0 = 6
-LAG = 2
+WARM0 = 3
+ACC_BANKS = 6
+NIMG = 3
+TLAG = 2
+DOT0 = 0
+DOT2 = 4
+COUNT = 6
+GLAG = 3
 
 
 def tile_partialconvolution_kernel(tc, x, seg_mask, conv_w, out):
@@ -40,28 +45,31 @@ def tile_partialconvolution_kernel(tc, x, seg_mask, conv_w, out):
     with ExitStack() as ctx:
         ctx.enter_context(tc.manual_schedule())
         const = ctx.enter_context(tc.tile_pool(name="const", bufs=1))
-        gpool = ctx.enter_context(tc.tile_pool(name="gated", bufs=16))
+        gpool = ctx.enter_context(tc.tile_pool(name="gated", bufs=20))
         xqpool = ctx.enter_context(tc.tile_pool(name="xquant", bufs=8))
         rpool = ctx.enter_context(tc.tile_pool(name="result", bufs=4))
         psum = ctx.enter_context(tc.psum_pool(name="psum", bufs=4))
 
         m0 = const.tile([P, 8, NCLS], BF16, name="m0")
-        xs = [const.tile([P, 4, CH], BF16, name="xs%d" % ip) for ip in range(2)]
+        xs = [const.tile([P, 2, CH], BF16, name="xs%d" % b) for b in range(4)]
+        v_parts = {ORDER[i]: V_PARTS[i] for i in range(TAPS)}
         wraw = [const.tile([P, 4, DIM], BF16, name="wraw%d" % k) for k in range(TAPS)]
 
         def load_w(k):
             nc.sync.dma_start(out=wraw[k][:], in_=wv[:, :, k, :])
 
-        def load_x(ip):
-            nc.sync.dma_start(out=xs[ip][:], in_=xv[:, 4 * ip : 4 * ip + 4, :])
+        def load_x(b):
+            nc.sync.dma_start(out=xs[b][:], in_=xv[:, 2 * b : 2 * b + 2, :])
 
         nc.sync.dma_start(out=m0[:], in_=sv)
-        load_w(0)
         load_x(0)
-        for k in range(1, 4):
-            load_w(k)
+        load_w(ORDER[0])
         load_x(1)
-        for k in range(4, TAPS):
+        load_w(ORDER[1])
+        load_x(2)
+        load_w(ORDER[2])
+        load_x(3)
+        for k in ORDER[3:]:
             load_w(k)
 
         zeros = const.tile([P, DIM], BF16, name="zeros")
@@ -71,7 +79,7 @@ def tile_partialconvolution_kernel(tc, x, seg_mask, conv_w, out):
             for i in range(times):
                 nc.tensor.matmul(out=dst, lhsT=zeros[:, 0:P], rhs=zeros[:, 0:width], start=True, stop=True)
 
-        warmt = psum.tile([P, DIM], F32, name="warmt", tag="tp")
+        warmt = psum.tile([P, DIM], F32, name="warmt", tag="tp", bufs=8 - ACC_BANKS)
         warm(warmt[:], WARM0)
         ident = const.tile([P, P], F32, name="ident")
         make_identity(nc, ident[:])
@@ -81,7 +89,7 @@ def tile_partialconvolution_kernel(tc, x, seg_mask, conv_w, out):
         w16 = wide[:, :, 128:256].rearrange("p j (a b) -> p j a b", b=16)
         nc.vector.memset(w16[:, 0, :, 0:1], 0.0)
         nc.vector.memset(w16[:, 2, :, 15:16], 0.0)
-        gq = [const.tile([P, 2, 4 * PIX], BF16, name="gq%d" % k, align_bytes=64) for k in range(TAPS)]
+        gq = [const.tile([P, NIMG, 4 * PIX], BF16, name="gq%d" % k, align_bytes=64) for k in range(TAPS)]
         shift = [16 * (k // 3 - 1) + k % 3 - 1 for k in range(TAPS)]
         for k in range(TAPS):
             if shift[k] < 0:
@@ -91,9 +99,11 @@ def tile_partialconvolution_kernel(tc, x, seg_mask, conv_w, out):
 
         mx0 = const.tile([P, 8], F32, name="mx0")
         e0 = const.tile([P, 8, NCLS], BF16, name="e0")
-        prod = const.tile([P, 2, TAPS, 4, NCLS], BF16, name="prod")
-        sels = const.tile([P, 2, TAPS, 4], F32, name="sels")
-        nz = const.tile([P, 2, TAPS, 4], BF16, name="nz")
+        eshs = const.tile([P, 3, 8, NCLS], BF16, name="eshs")
+        prod = const.tile([P, TAPS, 8, NCLS], BF16, name="prod")
+        sels = const.tile([P, TAPS, 8], F32, name="sels")
+        nz = const.tile([P, TAPS, 8], BF16, name="nz")
+        cnt = const.tile([P, 8], F32, name="cnt")
         cmax = const.tile([P, 8], F32, name="cmax")
         crec = const.tile([P, 8], F32, name="crec")
         norm = const.tile([P, 8], F32, name="norm")
@@ -104,10 +114,12 @@ def tile_partialconvolution_kernel(tc, x, seg_mask, conv_w, out):
         )
 
         def shift_onehot(tg):
-            esh = psum.tile([P, 3, 8, NCLS], BF16, name="esh", tag="acc")
+            esh = psum.tile([P, 3, 8, NCLS], BF16, name="esh", tag="acc", bufs=ACC_BANKS)
             di = tg - 1
             for kk in range(3):
                 sh = 16 * di + kk - 1
+                if sh == 0:
+                    continue
                 nc.tensor.matmul(
                     out=esh[:, kk, :, :],
                     lhsT=wide[:, kk, 128 - sh : 256 - sh],
@@ -133,35 +145,37 @@ def tile_partialconvolution_kernel(tc, x, seg_mask, conv_w, out):
                     )
             return esh
 
-        def dot_classes(ip, tg, esh):
-            ks = slice(3 * tg, 3 * tg + 3)
+        def dot_classes(ks, shifted):
+            n = len(range(ks.start, ks.stop, ks.step))
             nc.vector.tensor_tensor(
-                out=prod[:, ip, ks, :, :],
-                in0=esh[:, :, 4 * ip : 4 * ip + 4, :],
-                in1=m0[:, 4 * ip : 4 * ip + 4, :].unsqueeze(1).to_broadcast([P, 3, 4, NCLS]),
+                out=prod[:, ks, :, :],
+                in0=shifted,
+                in1=m0[:].unsqueeze(1).to_broadcast([P, n, 8, NCLS]),
                 op=ALU.mult,
             )
-            nc.vector.tensor_reduce(out=sels[:, ip, ks, :], in_=prod[:, ip, ks, :, :], axis=AX.X, op=ALU.add)
+            nc.vector.tensor_reduce(out=sels[:, ks, :], in_=prod[:, ks, :, :], axis=AX.X, op=ALU.add)
+
+        def nonzero():
+            nc.vector.tensor_single_scalar(out=nz[:], in_=sels[:], scalar=0.0, op=ALU.not_equal)
 
         def count_taps():
-            nc.vector.tensor_single_scalar(out=nz[:], in_=sels[:], scalar=0.0, op=ALU.not_equal)
-            cp = psum.tile([P, 2, 4], F32, name="cp", tag="acc")
+            cp = psum.tile([P, 8], F32, name="cp", tag="tp", bufs=8 - ACC_BANKS)
             steps = []
             for k in range(TAPS):
                 sh = shift[k]
-                steps.append((cp[:, :, :], 128 + sh, nz[:, :, k, :]))
+                steps.append((cp[:], 128 + sh, nz[:, k, :]))
                 if k >= 6:
-                    steps.append((cp[:, :, 0:4:2], sh, nz[:, :, k, 1:4:2]))
+                    steps.append((cp[:, 0:8:2], sh, nz[:, k, 1:8:2]))
                 if k < 3:
-                    steps.append((cp[:, :, 1:4:2], 256 + sh, nz[:, :, k, 0:4:2]))
+                    steps.append((cp[:, 1:8:2], 256 + sh, nz[:, k, 0:8:2]))
             for i, (o, c0, r) in enumerate(steps):
                 nc.tensor.matmul(
                     out=o, lhsT=wide[:, 1, c0 : c0 + P], rhs=r, start=(i == 0), stop=(i == len(steps) - 1)
                 )
-            return cp
+            nc.scalar.copy(out=cnt[:], in_=cp[:])
 
-        def make_norm(cp):
-            nc.vector.tensor_scalar_max(out=cmax[:], in0=cp[:].rearrange("p a b -> p (a b)"), scalar1=1.0)
+        def make_norm():
+            nc.vector.tensor_scalar_max(out=cmax[:], in0=cnt[:], scalar1=1.0)
             nc.vector.reciprocal(out=crec[:], in_=cmax[:])
             nc.vector.tensor_scalar_mul(out=norm[:], in0=crec[:], scalar1=9.0)
 
@@ -173,25 +187,25 @@ def tile_partialconvolution_kernel(tc, x, seg_mask, conv_w, out):
             n = DIM // parts
             dst = wg[k][:, part * n : (part + 1) * n, :].rearrange("p (c i) t -> p c t i", i=4)
             src = wraw[k][:, :, part * n : (part + 1) * n].rearrange("p t (c i) -> p c t i", i=4)
-            if k in W_ON_VECTOR:
+            if part < v_parts[k]:
                 nc.vector.tensor_copy(out=dst, in_=src)
             else:
                 nc.scalar.copy(out=dst, in_=src)
 
         def quantise_w(k):
-            if k in W_ON_VECTOR:
-                regroup_w(k, 0, 1)
+            for part in range(v_parts[k]):
+                regroup_w(k, part, WPARTS)
             nc.vector.quantize_mx(
                 out=wq[:, k, :].bitcast(FP8X4), scales=ws[:, k, :], in_=wg[k][:].rearrange("p d t -> p (d t)")
             )
 
-        xr = [const.tile([P, 4, CH], BF16, name="xr%d" % ip) for ip in range(2)]
+        xr = [const.tile([P, 2, CH], BF16, name="xr%d" % b) for b in range(4)]
 
-        def reorder_x(ip):
-            for m in range(4):
+        def reorder_x(b):
+            for mm in range(2):
                 nc.vector.tensor_copy(
-                    out=xr[ip][:, m, :].bitcast(F32).rearrange("p (u w) -> p u w", u=2),
-                    in_=xs[ip][:, m, :].bitcast(F32).rearrange("p (w u) -> p u w", u=2),
+                    out=xr[b][:, mm, :].bitcast(F32).rearrange("p (u w) -> p u w", u=2),
+                    in_=xs[b][:, mm, :].bitcast(F32).rearrange("p (w u) -> p u w", u=2),
                 )
 
         gts = {}
@@ -205,12 +219,12 @@ def tile_partialconvolution_kernel(tc, x, seg_mask, conv_w, out):
                 m = 2 * b + mm
                 gt = gpool.tile([P, CH], BF16, name="gt", tag="gt")
                 nc.vector.tensor_scalar_mul(
-                    out=gt[:], in0=xr[m // 4][:, m % 4, :], scalar1=sels[:, m // 4, k, m % 4 : m % 4 + 1]
+                    out=gt[:], in0=xr[b][:, mm, :], scalar1=sels[:, k, m : m + 1]
                 )
                 gts[(b, k, mm)] = gt
 
         def transpose(b, k):
-            pst = psum.tile([P, 2, PIX], F32, name="pst", tag="tp")
+            pst = psum.tile([P, 2, PIX], F32, name="pst", tag="tp", bufs=8 - ACC_BANKS)
             for mm in range(2):
                 words = gts[(b, k, mm)][:].bitcast(F32)
                 for u in range(2):
@@ -223,7 +237,7 @@ def tile_partialconvolution_kernel(tc, x, seg_mask, conv_w, out):
             sh = shift[k]
             d0, d1 = max(0, -sh), min(PIX, PIX - sh)
             nc.scalar.copy(
-                out=gq[k][:, b % 2, 4 * d0 : 4 * d1].bitcast(F32).rearrange("p (x u) -> p x u", u=2),
+                out=gq[k][:, b % NIMG, 4 * d0 : 4 * d1].bitcast(F32).rearrange("p (x u) -> p x u", u=2),
                 in_=psts[(b, k)][:, :, d0 + sh : d1 + sh].rearrange("p u x -> p x u"),
             )
 
@@ -231,74 +245,107 @@ def tile_partialconvolution_kernel(tc, x, seg_mask, conv_w, out):
             xq[(b, k)] = xqpool.tile([P, PIX], U32, name="xq", tag="xq", align_bytes=64)
             xsc[(b, k)] = xqpool.tile([P, PIX], U8, name="xsc", tag="xsc", align_bytes=64)
             nc.vector.quantize_mx(
-                out=xq[(b, k)][:].bitcast(FP8X4), scales=xsc[(b, k)][:], in_=gq[k][:, b % 2, :]
+                out=xq[(b, k)][:].bitcast(FP8X4), scales=xsc[(b, k)][:], in_=gq[k][:, b % NIMG, :]
             )
 
         def multiply(b, k):
             for mm in range(2):
-                if k == 0:
-                    acc[(b, mm)] = psum.tile([P, DIM], F32, name="acc", tag="acc")
+                if k == ORDER[0]:
+                    acc[(b, mm)] = psum.tile([P, DIM], F32, name="acc", tag="acc", bufs=ACC_BANKS)
                 nc.tensor.matmul_mx(
                     out=acc[(b, mm)][:],
                     lhsT=xq[(b, k)][:, mm * P : (mm + 1) * P].bitcast(FP8X4),
                     lhsT_scale=xsc[(b, k)][:, mm * P : (mm + 1) * P],
                     rhs=wq[:, k, :].bitcast(FP8X4),
                     rhs_scale=ws[:, k, :],
-                    start=(k == 0),
-                    stop=(k == TAPS - 1),
+                    start=(k == ORDER[0]),
+                    stop=(k == ORDER[-1]),
                 )
-                if k == TAPS - 1:
-                    m = 2 * b + mm
-                    res = rpool.tile([P, DIM], F32, name="res", tag="res")
-                    nc.scalar.activation(out=res[:], in_=acc[(b, mm)][:], func=ACTF.Copy, scale=norm[:, m : m + 1])
-                    nc.sync.dma_start(out=ov[m * P : (m + 1) * P, :], in_=res[:])
 
-        esh = [shift_onehot(tg) for tg in range(3)]
-        for k in S_HEAD:
-            for part in range(WPARTS):
-                regroup_w(k, part, WPARTS)
-        sfill = [(k, part) for k in S_FILL for part in range(WPARTS)]
-        for tg in range(3):
-            dot_classes(0, tg, esh[tg])
-        reorder_x(0)
+        def finish(b, mm, on_vector):
+            m = 2 * b + mm
+            res = rpool.tile([P, DIM], F32, name="res", tag="res")
+            if on_vector:
+                nc.vector.tensor_scalar_mul(out=res[:], in0=acc[(b, mm)][:], scalar1=norm[:, m : m + 1])
+            else:
+                nc.scalar.activation(out=res[:], in_=acc[(b, mm)][:], func=ACTF.Copy, scale=norm[:, m : m + 1])
+            nc.sync.dma_start(out=ov[m * P : (m + 1) * P, :], in_=res[:])
 
-        steps = [(ph, k) for ph in range(len(PHASES)) for k in range(TAPS)]
+        esh = {}
+        for tg in (1, 0, 2):
+            esh[tg] = shift_onehot(tg)
+        nc.scalar.copy(out=eshs[:], in_=esh[2][:])
+        sparts = [(k, part) for k in ORDER for part in range(v_parts[k], WPARTS)]
+
+        def fill(n):
+            for f in range(min(n, len(sparts))):
+                regroup_w(sparts[0][0], sparts[0][1], WPARTS)
+                sparts.remove(sparts[0])
+
+        units = []
+        for i in range(0, 8, 2):
+            for k in ORDER[i : i + 2]:
+                units.extend([(0, k), (1, k)])
+            for k in ORDER[i : i + 2]:
+                units.append((2, k))
+        units.extend([(b, ORDER[8]) for b in range(3)])
+        units.extend([(3, k) for k in ORDER])
+        chunks = [units[i : i + 2] for i in range(0, len(units), 2)]
+        quantised = []
 
         def front(j):
-            ph, k = steps[j]
-            for b in PHASES[ph]:
+            for b, k in chunks[j]:
                 gate(b, k)
 
         def middle(j):
-            ph, k = steps[j]
-            for b in PHASES[ph]:
+            for b, k in chunks[j]:
                 transpose(b, k)
-            for b in PHASES[ph]:
+            for b, k in chunks[j]:
                 evacuate(b, k)
-            for f in sfill[(FILL[j - 1] if 0 < j <= len(FILL) else 0 if j == 0 else 99) : (FILL[j] if j < len(FILL) else 99)]:
-                regroup_w(f[0], f[1], WPARTS)
 
-        def back(j):
-            ph, k = steps[j]
-            for b in PHASES[ph]:
-                multiply(b, k)
-
-        for j in range(LAG):
-            front(j)
-        for tg in range(3):
-            dot_classes(1, tg, esh[tg])
-        cp = count_taps()
-        for j in range(LAG):
-            middle(j)
-        make_norm(cp)
+        dot_classes(slice(4, 5, 1), e0[:].unsqueeze(1))
+        reorder_x(0)
+        gate(0, ORDER[0])
+        dot_classes(slice(3, 6, 2), esh[1][:, 0:3:2, :, :])
         reorder_x(1)
-        for j in range(len(steps)):
-            if j + LAG < len(steps):
-                front(j + LAG)
-                middle(j + LAG)
-            ph, k = steps[j]
-            for b in PHASES[ph]:
+        gate(1, ORDER[0])
+        fill(HEAD_PARTS)
+        for j in range(1, GLAG):
+            if j == 2:
+                reorder_x(2)
+            front(j)
+        for j in range(TLAG):
+            middle(j)
+        for j in range(len(chunks)):
+            if j + TLAG < len(chunks):
+                middle(j + TLAG)
+                fill(CHUNK_PARTS)
+            for b, k in chunks[j]:
+                if k not in quantised:
+                    quantise_w(k)
+                    quantised.append(k)
+            for b, k in chunks[j]:
                 quantise_x(b, k)
-            if ph == 0:
-                quantise_w(k)
-            back(j)
+            if j == DOT0:
+                dot_classes(slice(0, 3, 1), esh[0][:])
+            if j == DOT2:
+                dot_classes(slice(6, 9, 1), eshs[:])
+                nonzero()
+            if j == 0 and GLAG == 2:
+                reorder_x(2)
+            if j == 7:
+                reorder_x(3)
+            if j + GLAG < len(chunks):
+                front(j + GLAG)
+            for b, k in chunks[j]:
+                multiply(b, k)
+                if k == ORDER[-1] and b in (0, 3):
+                    finish(b, 0, False)
+                    finish(b, 1, b == 3)
+            if j in (14, 15):
+                finish(j - 13, 0, True)
+                finish(j - 13, 1, True)
+            if j == COUNT:
+                count_taps()
+            if j == COUNT + 1:
+                make_norm()

@@ -27,7 +27,6 @@ CHUNK_PARTS = 2
 WPARTS = 4
 WARM0 = 3
 ACC_BANKS = 6
-NIMG = 3
 TLAG = 2
 DOT0 = 0
 DOT2 = 4
@@ -46,7 +45,7 @@ def tile_partialconvolution_kernel(tc, x, seg_mask, conv_w, out):
         ctx.enter_context(tc.manual_schedule())
         const = ctx.enter_context(tc.tile_pool(name="const", bufs=1))
         gpool = ctx.enter_context(tc.tile_pool(name="gated", bufs=20))
-        xqpool = ctx.enter_context(tc.tile_pool(name="xquant", bufs=8))
+        xqpool = ctx.enter_context(tc.tile_pool(name="xquant", bufs=5))
         rpool = ctx.enter_context(tc.tile_pool(name="result", bufs=4))
         psum = ctx.enter_context(tc.psum_pool(name="psum", bufs=4))
 
@@ -89,13 +88,26 @@ def tile_partialconvolution_kernel(tc, x, seg_mask, conv_w, out):
         w16 = wide[:, :, 128:256].rearrange("p j (a b) -> p j a b", b=16)
         nc.vector.memset(w16[:, 0, :, 0:1], 0.0)
         nc.vector.memset(w16[:, 2, :, 15:16], 0.0)
-        gq = [const.tile([P, NIMG, 4 * PIX], BF16, name="gq%d" % k, align_bytes=64) for k in range(TAPS)]
         shift = [16 * (k // 3 - 1) + k % 3 - 1 for k in range(TAPS)]
-        for k in range(TAPS):
-            if shift[k] < 0:
-                nc.gpsimd.memset(gq[k][:, :, 0 : -4 * shift[k]], 0.0)
-            if shift[k] > 0:
-                nc.gpsimd.memset(gq[k][:, :, 4 * (PIX - shift[k]) : 4 * PIX], 0.0)
+
+        two_taps = [list(ORDER[i : i + 2]) for i in range(0, TAPS, 2)]
+        chunks = []
+        for ks in two_taps:
+            for k in ks:
+                chunks.append([(0, k), (1, k)])
+            chunks.append([(2, k) for k in ks])
+        for ks in two_taps:
+            chunks.append([(3, k) for k in ks])
+        gq = {}
+        for chunk in chunks:
+            ks = tuple(k for b, k in chunk)
+            if ks not in gq:
+                gq[ks] = const.tile([P, len(ks), 4 * PIX], BF16, name="gq%d" % len(gq), align_bytes=64)
+                for i, k in enumerate(ks):
+                    if shift[k] < 0:
+                        nc.vector.memset(gq[ks][:, i, 0 : -4 * shift[k]], 0.0)
+                    if shift[k] > 0:
+                        nc.vector.memset(gq[ks][:, i, 4 * (PIX - shift[k]) : 4 * PIX], 0.0)
 
         mx0 = const.tile([P, 8], F32, name="mx0")
         e0 = const.tile([P, 8, NCLS], BF16, name="e0")
@@ -183,18 +195,16 @@ def tile_partialconvolution_kernel(tc, x, seg_mask, conv_w, out):
         ws = const.tile([P, TAPS, DIM], U8, name="ws", align_bytes=64)
         wg = [const.tile([P, DIM, 4], BF16, name="wg%d" % k, align_bytes=64) for k in range(TAPS)]
 
-        def regroup_w(k, part, parts):
-            n = DIM // parts
-            dst = wg[k][:, part * n : (part + 1) * n, :].rearrange("p (c i) t -> p c t i", i=4)
-            src = wraw[k][:, :, part * n : (part + 1) * n].rearrange("p t (c i) -> p c t i", i=4)
-            if part < v_parts[k]:
-                nc.vector.tensor_copy(out=dst, in_=src)
-            else:
-                nc.scalar.copy(out=dst, in_=src)
+        def regroup_w(copy, k, part, end):
+            n = DIM // WPARTS
+            copy(
+                out=wg[k][:, part * n : end * n, :].rearrange("p (c i) t -> p c t i", i=4),
+                in_=wraw[k][:, :, part * n : end * n].rearrange("p t (c i) -> p c t i", i=4),
+            )
 
         def quantise_w(k):
-            for part in range(v_parts[k]):
-                regroup_w(k, part, WPARTS)
+            if v_parts[k] > 0:
+                regroup_w(nc.vector.tensor_copy, k, 0, v_parts[k])
             nc.vector.quantize_mx(
                 out=wq[:, k, :].bitcast(FP8X4), scales=ws[:, k, :], in_=wg[k][:].rearrange("p d t -> p (d t)")
             )
@@ -202,11 +212,10 @@ def tile_partialconvolution_kernel(tc, x, seg_mask, conv_w, out):
         xr = [const.tile([P, 2, CH], BF16, name="xr%d" % b) for b in range(4)]
 
         def reorder_x(b):
-            for mm in range(2):
-                nc.vector.tensor_copy(
-                    out=xr[b][:, mm, :].bitcast(F32).rearrange("p (u w) -> p u w", u=2),
-                    in_=xs[b][:, mm, :].bitcast(F32).rearrange("p (w u) -> p u w", u=2),
-                )
+            nc.vector.tensor_copy(
+                out=xr[b][:].bitcast(F32).rearrange("p m (u w) -> p m u w", u=2),
+                in_=xs[b][:].bitcast(F32).rearrange("p m (w u) -> p m u w", u=2),
+            )
 
         gts = {}
         psts = {}
@@ -233,20 +242,29 @@ def tile_partialconvolution_kernel(tc, x, seg_mask, conv_w, out):
                     )
             psts[(b, k)] = pst
 
-        def evacuate(b, k):
-            sh = shift[k]
-            d0, d1 = max(0, -sh), min(PIX, PIX - sh)
-            nc.scalar.copy(
-                out=gq[k][:, b % NIMG, 4 * d0 : 4 * d1].bitcast(F32).rearrange("p (x u) -> p x u", u=2),
-                in_=psts[(b, k)][:, :, d0 + sh : d1 + sh].rearrange("p u x -> p x u"),
-            )
+        def evacuate(chunk):
+            ks = tuple(k for b, k in chunk)
+            for i, (b, k) in enumerate(chunk):
+                sh = shift[k]
+                d0, d1 = max(0, -sh), min(PIX, PIX - sh)
+                nc.scalar.copy(
+                    out=gq[ks][:, i, 4 * d0 : 4 * d1].bitcast(F32).rearrange("p (x u) -> p x u", u=2),
+                    in_=psts[(b, k)][:, :, d0 + sh : d1 + sh].rearrange("p u x -> p x u"),
+                )
 
-        def quantise_x(b, k):
-            xq[(b, k)] = xqpool.tile([P, PIX], U32, name="xq", tag="xq", align_bytes=64)
-            xsc[(b, k)] = xqpool.tile([P, PIX], U8, name="xsc", tag="xsc", align_bytes=64)
+        def quantise_x(chunk):
+            ks = tuple(k for b, k in chunk)
+            q = xqpool.tile([P, 2, PIX], U32, name="xq", tag="xq", align_bytes=64)
+            s = xqpool.tile([P, 2, PIX], U8, name="xsc", tag="xsc", align_bytes=64)
+            n = len(chunk)
             nc.vector.quantize_mx(
-                out=xq[(b, k)][:].bitcast(FP8X4), scales=xsc[(b, k)][:], in_=gq[k][:, b % NIMG, :]
+                out=q[:, 0:n, :].rearrange("p i x -> p (i x)").bitcast(FP8X4),
+                scales=s[:, 0:n, :].rearrange("p i x -> p (i x)"),
+                in_=gq[ks][:].rearrange("p i w -> p (i w)"),
             )
+            for i, unit in enumerate(chunk):
+                xq[unit] = q[:, i, :]
+                xsc[unit] = s[:, i, :]
 
         def multiply(b, k):
             for mm in range(2):
@@ -279,18 +297,10 @@ def tile_partialconvolution_kernel(tc, x, seg_mask, conv_w, out):
 
         def fill(n):
             for f in range(min(n, len(sparts))):
-                regroup_w(sparts[0][0], sparts[0][1], WPARTS)
+                k, part = sparts[0]
+                regroup_w(nc.scalar.copy, k, part, part + 1)
                 sparts.remove(sparts[0])
 
-        units = []
-        for i in range(0, 8, 2):
-            for k in ORDER[i : i + 2]:
-                units.extend([(0, k), (1, k)])
-            for k in ORDER[i : i + 2]:
-                units.append((2, k))
-        units.extend([(b, ORDER[8]) for b in range(3)])
-        units.extend([(3, k) for k in ORDER])
-        chunks = [units[i : i + 2] for i in range(0, len(units), 2)]
         quantised = []
 
         def front(j):
@@ -300,8 +310,7 @@ def tile_partialconvolution_kernel(tc, x, seg_mask, conv_w, out):
         def middle(j):
             for b, k in chunks[j]:
                 transpose(b, k)
-            for b, k in chunks[j]:
-                evacuate(b, k)
+            evacuate(chunks[j])
 
         dot_classes(slice(4, 5, 1), e0[:].unsqueeze(1))
         reorder_x(0)
@@ -324,8 +333,7 @@ def tile_partialconvolution_kernel(tc, x, seg_mask, conv_w, out):
                 if k not in quantised:
                     quantise_w(k)
                     quantised.append(k)
-            for b, k in chunks[j]:
-                quantise_x(b, k)
+            quantise_x(chunks[j])
             if j == DOT0:
                 dot_classes(slice(0, 3, 1), esh[0][:])
             if j == DOT2:
@@ -342,9 +350,9 @@ def tile_partialconvolution_kernel(tc, x, seg_mask, conv_w, out):
                 if k == ORDER[-1] and b in (0, 3):
                     finish(b, 0, False)
                     finish(b, 1, b == 3)
-            if j in (14, 15):
-                finish(j - 13, 0, True)
-                finish(j - 13, 1, True)
+            if j in (15, 16):
+                finish(j - 14, 0, True)
+                finish(j - 14, 1, True)
             if j == COUNT:
                 count_taps()
             if j == COUNT + 1:

@@ -21,7 +21,7 @@ PIX = 256
 FLOPS = 2 * 1024 * 4608 * 512
 
 ORDER = (4, 3, 5, 0, 1, 2, 6, 7, 8)
-V_PARTS = (0, 4, 1, 1, 1, 1, 1, 1, 1)
+V_PARTS = (1, 3, 1, 1, 1, 1, 1, 1, 1)
 HEAD_PARTS = 4
 CHUNK_PARTS = 2
 WPARTS = 4
@@ -72,7 +72,7 @@ def tile_partialconvolution_kernel(tc, x, seg_mask, conv_w, out):
             load_w(k)
 
         zeros = const.tile([P, DIM], BF16, name="zeros")
-        nc.vector.memset(zeros[:], 0.0)
+        nc.vector.memset(zeros[:].bitcast(U32), 0)
 
         def warm(dst, times, width=DIM):
             for i in range(times):
@@ -83,7 +83,7 @@ def tile_partialconvolution_kernel(tc, x, seg_mask, conv_w, out):
         ident = const.tile([P, P], F32, name="ident")
         make_identity(nc, ident[:])
         wide = const.tile([P, 3, 384], BF16, name="wide")
-        nc.vector.memset(wide[:], 0.0)
+        nc.vector.memset(wide[:].bitcast(U32), 0)
         nc.vector.tensor_copy(out=wide[:, :, 128:256], in_=ident[:].unsqueeze(1).to_broadcast([P, 3, P]))
         w16 = wide[:, :, 128:256].rearrange("p j (a b) -> p j a b", b=16)
         nc.vector.memset(w16[:, 0, :, 0:1], 0.0)
@@ -103,11 +103,12 @@ def tile_partialconvolution_kernel(tc, x, seg_mask, conv_w, out):
             ks = tuple(k for b, k in chunk)
             if ks not in gq:
                 gq[ks] = const.tile([P, len(ks), 4 * PIX], BF16, name="gq%d" % len(gq), align_bytes=64)
-                for i, k in enumerate(ks):
+                for k in sorted(set(ks)):
+                    units = slice(ks.index(k), ks.index(k) + len([q for q in ks if q == k]))
                     if shift[k] < 0:
-                        nc.vector.memset(gq[ks][:, i, 0 : -4 * shift[k]], 0.0)
+                        nc.gpsimd.memset(gq[ks][:, units, 0 : -4 * shift[k]], 0.0)
                     if shift[k] > 0:
-                        nc.vector.memset(gq[ks][:, i, 4 * (PIX - shift[k]) : 4 * PIX], 0.0)
+                        nc.gpsimd.memset(gq[ks][:, units, 4 * (PIX - shift[k]) : 4 * PIX], 0.0)
 
         mx0 = const.tile([P, 8], F32, name="mx0")
         e0 = const.tile([P, 8, NCLS], BF16, name="e0")
@@ -116,8 +117,7 @@ def tile_partialconvolution_kernel(tc, x, seg_mask, conv_w, out):
         sels = const.tile([P, TAPS, 8], F32, name="sels")
         nz = const.tile([P, TAPS, 8], BF16, name="nz")
         cnt = const.tile([P, 8], F32, name="cnt")
-        cmax = const.tile([P, 8], F32, name="cmax")
-        crec = const.tile([P, 8], F32, name="crec")
+        ninth = const.tile([P, 8], F32, name="ninth")
         norm = const.tile([P, 8], F32, name="norm")
 
         nc.vector.tensor_reduce(out=mx0[:], in_=m0[:], axis=AX.X, op=ALU.max)
@@ -157,7 +157,7 @@ def tile_partialconvolution_kernel(tc, x, seg_mask, conv_w, out):
                     )
             return esh
 
-        def dot_classes(ks, shifted):
+        def mask_classes(ks, shifted):
             n = len(range(ks.start, ks.stop, ks.step))
             nc.vector.tensor_tensor(
                 out=prod[:, ks, :, :],
@@ -165,6 +165,8 @@ def tile_partialconvolution_kernel(tc, x, seg_mask, conv_w, out):
                 in1=m0[:].unsqueeze(1).to_broadcast([P, n, 8, NCLS]),
                 op=ALU.mult,
             )
+
+        def sum_classes(ks):
             nc.vector.tensor_reduce(out=sels[:, ks, :], in_=prod[:, ks, :, :], axis=AX.X, op=ALU.add)
 
         def nonzero():
@@ -186,10 +188,13 @@ def tile_partialconvolution_kernel(tc, x, seg_mask, conv_w, out):
                 )
             nc.scalar.copy(out=cnt[:], in_=cp[:])
 
+        def scale_count():
+            nc.vector.tensor_scalar(
+                out=ninth[:], in0=cnt[:], scalar1=1.0, scalar2=1.0 / 9.0, op0=ALU.max, op1=ALU.mult
+            )
+
         def make_norm():
-            nc.vector.tensor_scalar_max(out=cmax[:], in0=cnt[:], scalar1=1.0)
-            nc.vector.reciprocal(out=crec[:], in_=cmax[:])
-            nc.vector.tensor_scalar_mul(out=norm[:], in0=crec[:], scalar1=9.0)
+            nc.vector.reciprocal(out=norm[:], in_=ninth[:])
 
         wq = const.tile([P, TAPS, DIM], U32, name="wq", align_bytes=64)
         ws = const.tile([P, TAPS, DIM], U8, name="ws", align_bytes=64)
@@ -203,8 +208,6 @@ def tile_partialconvolution_kernel(tc, x, seg_mask, conv_w, out):
             )
 
         def quantise_w(k):
-            if v_parts[k] > 0:
-                regroup_w(nc.vector.tensor_copy, k, 0, v_parts[k])
             nc.vector.quantize_mx(
                 out=wq[:, k, :].bitcast(FP8X4), scales=ws[:, k, :], in_=wg[k][:].rearrange("p d t -> p (d t)")
             )
@@ -256,12 +259,8 @@ def tile_partialconvolution_kernel(tc, x, seg_mask, conv_w, out):
             ks = tuple(k for b, k in chunk)
             q = xqpool.tile([P, 2, PIX], U32, name="xq", tag="xq", align_bytes=64)
             s = xqpool.tile([P, 2, PIX], U8, name="xsc", tag="xsc", align_bytes=64)
-            n = len(chunk)
-            nc.vector.quantize_mx(
-                out=q[:, 0:n, :].rearrange("p i x -> p (i x)").bitcast(FP8X4),
-                scales=s[:, 0:n, :].rearrange("p i x -> p (i x)"),
-                in_=gq[ks][:].rearrange("p i w -> p (i w)"),
-            )
+            for i in range(len(chunk)):
+                nc.vector.quantize_mx(out=q[:, i, :].bitcast(FP8X4), scales=s[:, i, :], in_=gq[ks][:, i, :])
             for i, unit in enumerate(chunk):
                 xq[unit] = q[:, i, :]
                 xsc[unit] = s[:, i, :]
@@ -292,7 +291,6 @@ def tile_partialconvolution_kernel(tc, x, seg_mask, conv_w, out):
         esh = {}
         for tg in (1, 0, 2):
             esh[tg] = shift_onehot(tg)
-        nc.scalar.copy(out=eshs[:], in_=esh[2][:])
         sparts = [(k, part) for k in ORDER for part in range(v_parts[k], WPARTS)]
 
         def fill(n):
@@ -301,7 +299,6 @@ def tile_partialconvolution_kernel(tc, x, seg_mask, conv_w, out):
                 regroup_w(nc.scalar.copy, k, part, part + 1)
                 sparts.remove(sparts[0])
 
-        quantised = []
 
         def front(j):
             for b, k in chunks[j]:
@@ -312,39 +309,64 @@ def tile_partialconvolution_kernel(tc, x, seg_mask, conv_w, out):
                 transpose(b, k)
             evacuate(chunks[j])
 
-        dot_classes(slice(4, 5, 1), e0[:].unsqueeze(1))
+        def due(k):
+            return min(i for i, c in enumerate(chunks) if k in [u[1] for u in c])
+
+        def regroup_on_vector(j):
+            for k in first_taps[j] if j < len(chunks) else []:
+                if v_parts[k] > 0:
+                    regroup_w(nc.vector.tensor_copy, k, 0, v_parts[k])
+
+        first_taps = [[k for k in ORDER if due(k) == j] for j in range(len(chunks))]
+        rows = (slice(0, 3, 1), slice(3, 6, 2), slice(6, 9, 1))
+        mask_classes(slice(4, 5, 1), e0[:].unsqueeze(1))
         reorder_x(0)
+        sum_classes(slice(4, 5, 1))
+        mask_classes(rows[1], esh[1][:, 0:3:2, :, :])
         gate(0, ORDER[0])
-        dot_classes(slice(3, 6, 2), esh[1][:, 0:3:2, :, :])
+        sum_classes(rows[1])
         reorder_x(1)
+        regroup_on_vector(0)
         gate(1, ORDER[0])
         fill(HEAD_PARTS)
         for j in range(1, GLAG):
             if j == 2:
                 reorder_x(2)
+                regroup_on_vector(1)
             front(j)
         for j in range(TLAG):
             middle(j)
+        nc.scalar.copy(out=eshs[:], in_=esh[2][:])
         for j in range(len(chunks)):
             if j + TLAG < len(chunks):
                 middle(j + TLAG)
-                fill(CHUNK_PARTS)
-            for b, k in chunks[j]:
-                if k not in quantised:
-                    quantise_w(k)
-                    quantised.append(k)
+                fill(max(CHUNK_PARTS, len([p for p in sparts if due(p[0]) <= j + 1])))
+            for k in first_taps[j]:
+                quantise_w(k)
             quantise_x(chunks[j])
             if j == DOT0:
-                dot_classes(slice(0, 3, 1), esh[0][:])
+                mask_classes(rows[0], esh[0][:])
             if j == DOT2:
-                dot_classes(slice(6, 9, 1), eshs[:])
-                nonzero()
-            if j == 0 and GLAG == 2:
-                reorder_x(2)
+                mask_classes(rows[2], eshs[:])
+            if j == COUNT + 1:
+                scale_count()
             if j == 7:
                 reorder_x(3)
-            if j + GLAG < len(chunks):
-                front(j + GLAG)
+            ahead = chunks[j + GLAG] if j + GLAG < len(chunks) else []
+            for b, k in ahead[0:1]:
+                gate(b, k)
+            if j == DOT0:
+                sum_classes(rows[0])
+            if j == DOT2:
+                sum_classes(rows[2])
+            if j == COUNT + 1:
+                make_norm()
+            if j > 0:
+                regroup_on_vector(j + 1)
+            for b, k in ahead[1:]:
+                gate(b, k)
+            if j == DOT2:
+                nonzero()
             for b, k in chunks[j]:
                 multiply(b, k)
                 if k == ORDER[-1] and b in (0, 3):
@@ -355,5 +377,3 @@ def tile_partialconvolution_kernel(tc, x, seg_mask, conv_w, out):
                 finish(j - 14, 1, True)
             if j == COUNT:
                 count_taps()
-            if j == COUNT + 1:
-                make_norm()

@@ -21,9 +21,8 @@ PIX = 256
 FLOPS = 2 * 1024 * 4608 * 512
 
 ORDER = (4, 3, 5, 0, 1, 2, 6, 7, 8)
-V_PARTS = (1, 3, 1, 1, 1, 1, 1, 1, 1)
-HEAD_PARTS = 4
-CHUNK_PARTS = 2
+V_PARTS = (1, 4, 2, 2, 2, 2, 2, 2, 2)
+HEAD_PARTS = 3
 WPARTS = 4
 WARM0 = 3
 ACC_BANKS = 6
@@ -212,14 +211,6 @@ def tile_partialconvolution_kernel(tc, x, seg_mask, conv_w, out):
                 out=wq[:, k, :].bitcast(FP8X4), scales=ws[:, k, :], in_=wg[k][:].rearrange("p d t -> p (d t)")
             )
 
-        xr = [const.tile([P, 2, CH], BF16, name="xr%d" % b) for b in range(4)]
-
-        def reorder_x(b):
-            nc.vector.tensor_copy(
-                out=xr[b][:].bitcast(F32).rearrange("p m (u w) -> p m u w", u=2),
-                in_=xs[b][:].bitcast(F32).rearrange("p m (w u) -> p m u w", u=2),
-            )
-
         gts = {}
         psts = {}
         xq = {}
@@ -231,7 +222,9 @@ def tile_partialconvolution_kernel(tc, x, seg_mask, conv_w, out):
                 m = 2 * b + mm
                 gt = gpool.tile([P, CH], BF16, name="gt", tag="gt")
                 nc.vector.tensor_scalar_mul(
-                    out=gt[:], in0=xr[b][:, mm, :], scalar1=sels[:, k, m : m + 1]
+                    out=gt[:].rearrange("p (u w e) -> p u w e", u=2, e=2),
+                    in0=xs[b][:, mm, :].rearrange("p (w u e) -> p u w e", u=2, e=2),
+                    scalar1=sels[:, k, m : m + 1],
                 )
                 gts[(b, k, mm)] = gt
 
@@ -320,18 +313,15 @@ def tile_partialconvolution_kernel(tc, x, seg_mask, conv_w, out):
         first_taps = [[k for k in ORDER if due(k) == j] for j in range(len(chunks))]
         rows = (slice(0, 3, 1), slice(3, 6, 2), slice(6, 9, 1))
         mask_classes(slice(4, 5, 1), e0[:].unsqueeze(1))
-        reorder_x(0)
         sum_classes(slice(4, 5, 1))
         mask_classes(rows[1], esh[1][:, 0:3:2, :, :])
         gate(0, ORDER[0])
         sum_classes(rows[1])
-        reorder_x(1)
         regroup_on_vector(0)
         gate(1, ORDER[0])
         fill(HEAD_PARTS)
         for j in range(1, GLAG):
             if j == 2:
-                reorder_x(2)
                 regroup_on_vector(1)
             front(j)
         for j in range(TLAG):
@@ -340,7 +330,7 @@ def tile_partialconvolution_kernel(tc, x, seg_mask, conv_w, out):
         for j in range(len(chunks)):
             if j + TLAG < len(chunks):
                 middle(j + TLAG)
-                fill(max(CHUNK_PARTS, len([p for p in sparts if due(p[0]) <= j + 1])))
+                fill(max([-(-len([p for p in sparts if due(p[0]) - 1 <= j + i]) // i) for i in range(1, 12)]))
             for k in first_taps[j]:
                 quantise_w(k)
             quantise_x(chunks[j])
@@ -348,10 +338,8 @@ def tile_partialconvolution_kernel(tc, x, seg_mask, conv_w, out):
                 mask_classes(rows[0], esh[0][:])
             if j == DOT2:
                 mask_classes(rows[2], eshs[:])
-            if j == COUNT + 1:
+            if j == COUNT + 2:
                 scale_count()
-            if j == 7:
-                reorder_x(3)
             ahead = chunks[j + GLAG] if j + GLAG < len(chunks) else []
             for b, k in ahead[0:1]:
                 gate(b, k)
@@ -359,7 +347,7 @@ def tile_partialconvolution_kernel(tc, x, seg_mask, conv_w, out):
                 sum_classes(rows[0])
             if j == DOT2:
                 sum_classes(rows[2])
-            if j == COUNT + 1:
+            if j == COUNT + 2:
                 make_norm()
             if j > 0:
                 regroup_on_vector(j + 1)

@@ -29,7 +29,7 @@ ACC_BANKS = 6
 TLAG = 2
 DOT0 = 0
 DOT2 = 4
-COUNT = 6
+COUNT = 5
 GLAG = 3
 
 
@@ -44,8 +44,8 @@ def tile_partialconvolution_kernel(tc, x, seg_mask, conv_w, out):
         ctx.enter_context(tc.manual_schedule())
         const = ctx.enter_context(tc.tile_pool(name="const", bufs=1))
         gpool = ctx.enter_context(tc.tile_pool(name="gated", bufs=20))
-        xqpool = ctx.enter_context(tc.tile_pool(name="xquant", bufs=5))
-        rpool = ctx.enter_context(tc.tile_pool(name="result", bufs=4))
+        xqpool = ctx.enter_context(tc.tile_pool(name="xquant", bufs=14))
+        rpool = ctx.enter_context(tc.tile_pool(name="result", bufs=6))
         psum = ctx.enter_context(tc.psum_pool(name="psum", bufs=4))
 
         m0 = const.tile([P, 8, NCLS], BF16, name="m0")
@@ -89,25 +89,19 @@ def tile_partialconvolution_kernel(tc, x, seg_mask, conv_w, out):
         nc.vector.memset(w16[:, 2, :, 15:16], 0.0)
         shift = [16 * (k // 3 - 1) + k % 3 - 1 for k in range(TAPS)]
 
-        two_taps = [list(ORDER[i : i + 2]) for i in range(0, TAPS, 2)]
         chunks = []
-        for ks in two_taps:
+        for i in range(0, TAPS, 2):
+            ks = ORDER[i : i + 2]
             for k in ks:
                 chunks.append([(0, k), (1, k)])
-            chunks.append([(2, k) for k in ks])
-        for ks in two_taps:
-            chunks.append([(3, k) for k in ks])
-        gq = {}
-        for chunk in chunks:
-            ks = tuple(k for b, k in chunk)
-            if ks not in gq:
-                gq[ks] = const.tile([P, len(ks), 4 * PIX], BF16, name="gq%d" % len(gq), align_bytes=64)
-                for k in sorted(set(ks)):
-                    units = slice(ks.index(k), ks.index(k) + len([q for q in ks if q == k]))
-                    if shift[k] < 0:
-                        nc.gpsimd.memset(gq[ks][:, units, 0 : -4 * shift[k]], 0.0)
-                    if shift[k] > 0:
-                        nc.gpsimd.memset(gq[ks][:, units, 4 * (PIX - shift[k]) : 4 * PIX], 0.0)
+            if len(ks) == 2:
+                chunks.append([(2, k) for k in ks])
+        gq = [const.tile([P, 3, 4 * PIX], BF16, name="gq%d" % k, align_bytes=64) for k in range(TAPS)]
+        for k in ORDER:
+            if shift[k] < 0:
+                nc.gpsimd.memset(gq[k][:, :, 0 : -4 * shift[k]], 0.0)
+            if shift[k] > 0:
+                nc.gpsimd.memset(gq[k][:, :, 4 * (PIX - shift[k]) : 4 * PIX], 0.0)
 
         mx0 = const.tile([P, 8], F32, name="mx0")
         e0 = const.tile([P, 8, NCLS], BF16, name="e0")
@@ -228,8 +222,8 @@ def tile_partialconvolution_kernel(tc, x, seg_mask, conv_w, out):
                 )
                 gts[(b, k, mm)] = gt
 
-        def transpose(b, k):
-            pst = psum.tile([P, 2, PIX], F32, name="pst", tag="tp", bufs=8 - ACC_BANKS)
+        def transpose(b, k, tag="tp"):
+            pst = psum.tile([P, 2, PIX], F32, name="pst", tag=tag, bufs=ACC_BANKS if tag == "acc" else 8 - ACC_BANKS)
             for mm in range(2):
                 words = gts[(b, k, mm)][:].bitcast(F32)
                 for u in range(2):
@@ -238,28 +232,22 @@ def tile_partialconvolution_kernel(tc, x, seg_mask, conv_w, out):
                     )
             psts[(b, k)] = pst
 
-        def evacuate(chunk):
-            ks = tuple(k for b, k in chunk)
-            for i, (b, k) in enumerate(chunk):
-                sh = shift[k]
-                d0, d1 = max(0, -sh), min(PIX, PIX - sh)
-                nc.scalar.copy(
-                    out=gq[ks][:, i, 4 * d0 : 4 * d1].bitcast(F32).rearrange("p (x u) -> p x u", u=2),
-                    in_=psts[(b, k)][:, :, d0 + sh : d1 + sh].rearrange("p u x -> p x u"),
-                )
+        def evacuate(b, k):
+            sh = shift[k]
+            d0, d1 = max(0, -sh), min(PIX, PIX - sh)
+            nc.scalar.copy(
+                out=gq[k][:, b % 3, 4 * d0 : 4 * d1].bitcast(F32).rearrange("p (x u) -> p x u", u=2),
+                in_=psts[(b, k)][:, :, d0 + sh : d1 + sh].rearrange("p u x -> p x u"),
+            )
 
-        def quantise_x(chunk):
-            ks = tuple(k for b, k in chunk)
-            q = xqpool.tile([P, 2, PIX], U32, name="xq", tag="xq", align_bytes=64)
-            s = xqpool.tile([P, 2, PIX], U8, name="xsc", tag="xsc", align_bytes=64)
-            for i in range(len(chunk)):
-                nc.vector.quantize_mx(out=q[:, i, :].bitcast(FP8X4), scales=s[:, i, :], in_=gq[ks][:, i, :])
-            for i, unit in enumerate(chunk):
-                xq[unit] = q[:, i, :]
-                xsc[unit] = s[:, i, :]
+        def quantise_x(b, k):
+            q = xqpool.tile([P, PIX], U32, name="xq", tag="xq", align_bytes=64)
+            s = xqpool.tile([P, PIX], U8, name="xsc", tag="xsc", align_bytes=64)
+            nc.vector.quantize_mx(out=q[:].bitcast(FP8X4), scales=s[:], in_=gq[k][:, b % 3, :])
+            xq[(b, k)], xsc[(b, k)] = q, s
 
-        def multiply(b, k):
-            for mm in range(2):
+        def multiply(b, k, mms=(0, 1)):
+            for mm in mms:
                 if k == ORDER[0]:
                     acc[(b, mm)] = psum.tile([P, DIM], F32, name="acc", tag="acc", bufs=ACC_BANKS)
                 nc.tensor.matmul_mx(
@@ -293,14 +281,19 @@ def tile_partialconvolution_kernel(tc, x, seg_mask, conv_w, out):
                 sparts.remove(sparts[0])
 
 
-        def front(j):
-            for b, k in chunks[j]:
+        def front(units):
+            for b, k in units:
                 gate(b, k)
 
-        def middle(j):
-            for b, k in chunks[j]:
-                transpose(b, k)
-            evacuate(chunks[j])
+        def middle(units, tag="tp"):
+            for b, k in units:
+                transpose(b, k, tag)
+            for b, k in units:
+                evacuate(b, k)
+
+        def back(units):
+            for b, k in units:
+                quantise_x(b, k)
 
         def due(k):
             return min(i for i, c in enumerate(chunks) if k in [u[1] for u in c])
@@ -323,26 +316,25 @@ def tile_partialconvolution_kernel(tc, x, seg_mask, conv_w, out):
         for j in range(1, GLAG):
             if j == 2:
                 regroup_on_vector(1)
-            front(j)
+            front(chunks[j])
         for j in range(TLAG):
-            middle(j)
+            middle(chunks[j])
         nc.scalar.copy(out=eshs[:], in_=esh[2][:])
+        last = [(3, k) for k in ORDER]
+        turns = chunks + [[(2, ORDER[-1]), last[0]], last[1:3], last[3:5]]
         for j in range(len(chunks)):
-            if j + TLAG < len(chunks):
-                middle(j + TLAG)
-                fill(max([-(-len([p for p in sparts if due(p[0]) - 1 <= j + i]) // i) for i in range(1, 12)]))
+            middle(turns[j + TLAG])
+            fill(max([-(-len([p for p in sparts if due(p[0]) - 1 <= j + i]) // i) for i in range(1, 12)]))
             for k in first_taps[j]:
                 quantise_w(k)
-            quantise_x(chunks[j])
+            back(chunks[j])
             if j == DOT0:
                 mask_classes(rows[0], esh[0][:])
             if j == DOT2:
                 mask_classes(rows[2], eshs[:])
             if j == COUNT + 2:
                 scale_count()
-            ahead = chunks[j + GLAG] if j + GLAG < len(chunks) else []
-            for b, k in ahead[0:1]:
-                gate(b, k)
+            front(turns[j + GLAG][0:1])
             if j == DOT0:
                 sum_classes(rows[0])
             if j == DOT2:
@@ -351,17 +343,37 @@ def tile_partialconvolution_kernel(tc, x, seg_mask, conv_w, out):
                 make_norm()
             if j > 0:
                 regroup_on_vector(j + 1)
-            for b, k in ahead[1:]:
-                gate(b, k)
+            front(turns[j + GLAG][1:2])
             if j == DOT2:
                 nonzero()
             for b, k in chunks[j]:
                 multiply(b, k)
-                if k == ORDER[-1] and b in (0, 3):
-                    finish(b, 0, False)
-                    finish(b, 1, b == 3)
-            if j in (15, 16):
-                finish(j - 14, 0, True)
-                finish(j - 14, 1, True)
             if j == COUNT:
                 count_taps()
+        for mm in range(2):
+            finish(0, mm, False)
+        middle(turns[15])
+        for mm in range(2):
+            finish(1, mm, False)
+        back(turns[13])
+        front(last[5:9])
+        back(turns[14])
+        for b, k in turns[13] + turns[14]:
+            multiply(b, k)
+        back(turns[15])
+        for mm in range(2):
+            finish(2, mm, True)
+        middle(last[5:9], "acc")
+        back(last[5:9])
+        for b, k in last[3:5]:
+            multiply(b, k)
+        for mm in range(2):
+            for b, k in last[5:9]:
+                multiply(b, k, (mm,))
+            if mm == 0:
+                finish(3, 0, False)
+        for h in range(2):
+            half = slice(h * (DIM // 2), (h + 1) * (DIM // 2))
+            res = rpool.tile([P, DIM // 2], F32, name="half", tag="half")
+            nc.scalar.activation(out=res[:], in_=acc[(3, 1)][:, half], func=ACTF.Copy, scale=norm[:, 7:8])
+            nc.sync.dma_start(out=ov[7 * P : 8 * P, half], in_=res[:])

@@ -21,9 +21,9 @@ PIX = 256
 FLOPS = 2 * 1024 * 4608 * 512
 
 ORDER = (4, 3, 5, 0, 1, 2, 6, 7, 8)
-V_PARTS = (1, 4, 2, 2, 2, 2, 2, 2, 2)
-HEAD_PARTS = 3
-WPARTS = 4
+V_PARTS = (2, 8, 4, 3, 4, 3, 4, 3, 4)
+HEAD_PARTS = 6
+WPARTS = 8
 WARM0 = 3
 ACC_BANKS = 6
 TLAG = 2
@@ -48,7 +48,8 @@ def tile_partialconvolution_kernel(tc, x, seg_mask, conv_w, out):
         rpool = ctx.enter_context(tc.tile_pool(name="result", bufs=6))
         psum = ctx.enter_context(tc.psum_pool(name="psum", bufs=4))
 
-        m0 = const.tile([P, 8, NCLS], BF16, name="m0")
+        m0rows = const.tile([P, 8, 32], BF16, name="m0rows", align_bytes=64)
+        m0 = m0rows[:, :, 0:NCLS]
         xs = [const.tile([P, 2, CH], BF16, name="xs%d" % b) for b in range(4)]
         v_parts = {ORDER[i]: V_PARTS[i] for i in range(TAPS)}
         wraw = [const.tile([P, 4, DIM], BF16, name="wraw%d" % k) for k in range(TAPS)]
@@ -59,7 +60,7 @@ def tile_partialconvolution_kernel(tc, x, seg_mask, conv_w, out):
         def load_x(b):
             nc.sync.dma_start(out=xs[b][:], in_=xv[:, 2 * b : 2 * b + 2, :])
 
-        nc.sync.dma_start(out=m0[:], in_=sv)
+        nc.sync.dma_start(out=m0, in_=sv)
         load_x(0)
         load_w(ORDER[0])
         load_x(1)
@@ -113,9 +114,9 @@ def tile_partialconvolution_kernel(tc, x, seg_mask, conv_w, out):
         ninth = const.tile([P, 8], F32, name="ninth")
         norm = const.tile([P, 8], F32, name="norm")
 
-        nc.vector.tensor_reduce(out=mx0[:], in_=m0[:], axis=AX.X, op=ALU.max)
+        nc.vector.tensor_reduce(out=mx0[:], in_=m0, axis=AX.X, op=ALU.max)
         nc.vector.tensor_tensor(
-            out=e0[:], in0=m0[:], in1=mx0[:].unsqueeze(2).to_broadcast([P, 8, NCLS]), op=ALU.is_equal
+            out=e0[:], in0=m0, in1=mx0[:].unsqueeze(2).to_broadcast([P, 8, NCLS]), op=ALU.is_equal
         )
 
         def shift_onehot(tg):
@@ -155,7 +156,7 @@ def tile_partialconvolution_kernel(tc, x, seg_mask, conv_w, out):
             nc.vector.tensor_tensor(
                 out=prod[:, ks, :, :],
                 in0=shifted,
-                in1=m0[:].unsqueeze(1).to_broadcast([P, n, 8, NCLS]),
+                in1=m0.unsqueeze(1).to_broadcast([P, n, 8, NCLS]),
                 op=ALU.mult,
             )
 

@@ -54,21 +54,24 @@ def tile_partialconvolution_kernel(tc, x, seg_mask, conv_w, out):
         v_parts = {ORDER[i]: V_PARTS[i] for i in range(TAPS)}
         wraw = [const.tile([P, 4, DIM], BF16, name="wraw%d" % k) for k in range(TAPS)]
 
-        def load_w(k):
-            nc.sync.dma_start(out=wraw[k][:], in_=wv[:, :, k, :])
+        def load_w(k, c0=0, c1=DIM):
+            nc.sync.dma_start(out=wraw[k][:, :, c0:c1], in_=wv[:, :, k, c0:c1])
 
         def load_x(b):
             nc.sync.dma_start(out=xs[b][:], in_=xv[:, 2 * b : 2 * b + 2, :])
 
         nc.sync.dma_start(out=m0, in_=sv)
+        load_w(ORDER[0], 0, DIM // 2)
         load_x(0)
-        load_w(ORDER[0])
+        load_w(ORDER[0], DIM // 2, DIM)
         load_x(1)
-        load_w(ORDER[1])
         load_x(2)
+        load_w(ORDER[1])
         load_w(ORDER[2])
+        for k in ORDER[3:5]:
+            load_w(k)
         load_x(3)
-        for k in ORDER[3:]:
+        for k in ORDER[5:]:
             load_w(k)
 
         zeros = const.tile([P, DIM], BF16, name="zeros")
@@ -114,10 +117,16 @@ def tile_partialconvolution_kernel(tc, x, seg_mask, conv_w, out):
         ninth = const.tile([P, 8], F32, name="ninth")
         norm = const.tile([P, 8], F32, name="norm")
 
-        nc.vector.tensor_reduce(out=mx0[:], in_=m0, axis=AX.X, op=ALU.max)
-        nc.vector.tensor_tensor(
-            out=e0[:], in0=m0, in1=mx0[:].unsqueeze(2).to_broadcast([P, 8, NCLS]), op=ALU.is_equal
-        )
+        halves = (slice(0, 4), slice(4, 8))
+        for ms in halves:
+            nc.vector.tensor_reduce(out=mx0[:, ms], in_=m0[:, ms, :], axis=AX.X, op=ALU.max)
+        for ms in halves:
+            nc.vector.tensor_tensor(
+                out=e0[:, ms, :],
+                in0=m0[:, ms, :],
+                in1=mx0[:, ms].unsqueeze(2).to_broadcast([P, 4, NCLS]),
+                op=ALU.is_equal,
+            )
 
         def shift_onehot(tg):
             esh = psum.tile([P, 3, 8, NCLS], BF16, name="esh", tag="acc", bufs=ACC_BANKS)
@@ -273,7 +282,7 @@ def tile_partialconvolution_kernel(tc, x, seg_mask, conv_w, out):
         esh = {}
         for tg in (1, 0, 2):
             esh[tg] = shift_onehot(tg)
-        sparts = [(k, part) for k in ORDER for part in range(v_parts[k], WPARTS)]
+        sparts = [(k, part) for k in ORDER for part in range(WPARTS - v_parts[k])]
 
         def fill(n):
             for f in range(min(n, len(sparts))):
@@ -302,12 +311,14 @@ def tile_partialconvolution_kernel(tc, x, seg_mask, conv_w, out):
         def regroup_on_vector(j):
             for k in first_taps[j] if j < len(chunks) else []:
                 if v_parts[k] > 0:
-                    regroup_w(nc.vector.tensor_copy, k, 0, v_parts[k])
+                    regroup_w(nc.vector.tensor_copy, k, WPARTS - v_parts[k], WPARTS)
 
         first_taps = [[k for k in ORDER if due(k) == j] for j in range(len(chunks))]
         rows = (slice(0, 3, 1), slice(3, 6, 2), slice(6, 9, 1))
-        mask_classes(slice(4, 5, 1), e0[:].unsqueeze(1))
-        sum_classes(slice(4, 5, 1))
+        for ms in halves:
+            nc.vector.tensor_tensor(out=prod[:, 4, ms, :], in0=e0[:, ms, :], in1=m0[:, ms, :], op=ALU.mult)
+        for ms in halves:
+            nc.vector.tensor_reduce(out=sels[:, 4, ms], in_=prod[:, 4, ms, :], axis=AX.X, op=ALU.add)
         mask_classes(rows[1], esh[1][:, 0:3:2, :, :])
         gate(0, ORDER[0])
         sum_classes(rows[1])
@@ -315,8 +326,6 @@ def tile_partialconvolution_kernel(tc, x, seg_mask, conv_w, out):
         gate(1, ORDER[0])
         fill(HEAD_PARTS)
         for j in range(1, GLAG):
-            if j == 2:
-                regroup_on_vector(1)
             front(chunks[j])
         for j in range(TLAG):
             middle(chunks[j])
@@ -329,6 +338,8 @@ def tile_partialconvolution_kernel(tc, x, seg_mask, conv_w, out):
             for k in first_taps[j]:
                 quantise_w(k)
             back(chunks[j])
+            if j == 0:
+                regroup_on_vector(1)
             if j == DOT0:
                 mask_classes(rows[0], esh[0][:])
             if j == DOT2:

from contextlib import ExitStack

import concourse.mybir as mybir
from concourse.masks import make_identity

F32 = mybir.dt.float32
BF16 = mybir.dt.bfloat16
U32 = mybir.dt.uint32
U8 = mybir.dt.uint8
FP8X4 = mybir.dt.float8_e4m3fn_x4
ALU = mybir.AluOpType
ACTF = mybir.ActivationFunctionType
AX = mybir.AxisListType

P = 128
NCLS = 22
TAPS = 9
DIM = 512
CH = 512
PIX = 256
FLOPS = 2 * 1024 * 4608 * 512

ORDER = (4, 3, 5, 0, 1, 2, 6, 7, 8)
V_PARTS = (2, 8, 4, 3, 4, 3, 4, 3, 4)
HEAD_PARTS = 6
WPARTS = 8
WARM0 = 3
ACC_BANKS = 6
TLAG = 2
DOT0 = 0
DOT2 = 4
COUNT = 5
GLAG = 3


def tile_partialconvolution_kernel(tc, x, seg_mask, conv_w, out):
    nc = tc.nc
    xv = x.rearrange("b h w c -> (b h w) c").rearrange("(m p) c -> p m c", p=P)
    sv = seg_mask.rearrange("b h w c -> (b h w) c").rearrange("(m p) c -> p m c", p=P)
    wv = conv_w.rearrange("(p t) i j d -> p t (i j) d", t=4)
    ov = out.rearrange("b h w d -> (b h w) d")

    with ExitStack() as ctx:
        ctx.enter_context(tc.manual_schedule())
        const = ctx.enter_context(tc.tile_pool(name="const", bufs=1))
        gpool = ctx.enter_context(tc.tile_pool(name="gated", bufs=20))
        xqpool = ctx.enter_context(tc.tile_pool(name="xquant", bufs=14))
        rpool = ctx.enter_context(tc.tile_pool(name="result", bufs=6))
        psum = ctx.enter_context(tc.psum_pool(name="psum", bufs=4))

        m0rows = const.tile([P, 8, 32], BF16, name="m0rows", align_bytes=64)
        m0 = m0rows[:, :, 0:NCLS]
        xs = [const.tile([P, 2, CH], BF16, name="xs%d" % b) for b in range(4)]
        v_parts = {ORDER[i]: V_PARTS[i] for i in range(TAPS)}
        wraw = [const.tile([P, 4, DIM], BF16, name="wraw%d" % k) for k in range(TAPS)]

        def load_w(k, c0=0, c1=DIM):
            nc.sync.dma_start(out=wraw[k][:, :, c0:c1], in_=wv[:, :, k, c0:c1])

        def load_x(b):
            nc.sync.dma_start(out=xs[b][:], in_=xv[:, 2 * b : 2 * b + 2, :])

        nc.sync.dma_start(out=m0, in_=sv)
        load_w(ORDER[0], 0, DIM // 2)
        load_x(0)
        load_w(ORDER[0], DIM // 2, DIM)
        load_x(1)
        load_x(2)
        load_w(ORDER[1])
        load_w(ORDER[2])
        for k in ORDER[3:5]:
            load_w(k)
        load_x(3)
        for k in ORDER[5:]:
            load_w(k)

        zeros = const.tile([P, DIM], BF16, name="zeros")
        nc.vector.memset(zeros[:].bitcast(U32), 0)

        def warm(dst, times, width=DIM):
            for i in range(times):
                nc.tensor.matmul(out=dst, lhsT=zeros[:, 0:P], rhs=zeros[:, 0:width], start=True, stop=True)

        warmt = psum.tile([P, DIM], F32, name="warmt", tag="tp", bufs=8 - ACC_BANKS)
        warm(warmt[:], WARM0)
        ident = const.tile([P, P], F32, name="ident")
        make_identity(nc, ident[:])
        wide = const.tile([P, 3, 384], BF16, name="wide")
        nc.vector.memset(wide[:].bitcast(U32), 0)
        nc.vector.tensor_copy(out=wide[:, :, 128:256], in_=ident[:].unsqueeze(1).to_broadcast([P, 3, P]))
        w16 = wide[:, :, 128:256].rearrange("p j (a b) -> p j a b", b=16)
        nc.vector.memset(w16[:, 0, :, 0:1], 0.0)
        nc.vector.memset(w16[:, 2, :, 15:16], 0.0)
        shift = [16 * (k // 3 - 1) + k % 3 - 1 for k in range(TAPS)]

        chunks = []
        for i in range(0, TAPS, 2):
            ks = ORDER[i : i + 2]
            for k in ks:
                chunks.append([(0, k), (1, k)])
            if len(ks) == 2:
                chunks.append([(2, k) for k in ks])
        gq = [const.tile([P, 3, 4 * PIX], BF16, name="gq%d" % k, align_bytes=64) for k in range(TAPS)]
        for k in ORDER:
            if shift[k] < 0:
                nc.gpsimd.memset(gq[k][:, :, 0 : -4 * shift[k]], 0.0)
            if shift[k] > 0:
                nc.gpsimd.memset(gq[k][:, :, 4 * (PIX - shift[k]) : 4 * PIX], 0.0)

        mx0 = const.tile([P, 8], F32, name="mx0")
        e0 = const.tile([P, 8, NCLS], BF16, name="e0")
        eshs = const.tile([P, 3, 8, NCLS], BF16, name="eshs")
        prod = const.tile([P, TAPS, 8, NCLS], BF16, name="prod")
        sels = const.tile([P, TAPS, 8], F32, name="sels")
        nz = const.tile([P, TAPS, 8], BF16, name="nz")
        cnt = const.tile([P, 8], F32, name="cnt")
        ninth = const.tile([P, 8], F32, name="ninth")
        norm = const.tile([P, 8], F32, name="norm")

        halves = (slice(0, 4), slice(4, 8))
        for ms in halves:
            nc.vector.tensor_reduce(out=mx0[:, ms], in_=m0[:, ms, :], axis=AX.X, op=ALU.max)
        for ms in halves:
            nc.vector.tensor_tensor(
                out=e0[:, ms, :],
                in0=m0[:, ms, :],
                in1=mx0[:, ms].unsqueeze(2).to_broadcast([P, 4, NCLS]),
                op=ALU.is_equal,
            )

        def shift_onehot(tg):
            esh = psum.tile([P, 3, 8, NCLS], BF16, name="esh", tag="acc", bufs=ACC_BANKS)
            di = tg - 1
            for kk in range(3):
                sh = 16 * di + kk - 1
                if sh == 0:
                    continue
                nc.tensor.matmul(
                    out=esh[:, kk, :, :],
                    lhsT=wide[:, kk, 128 - sh : 256 - sh],
                    rhs=e0[:],
                    start=True,
                    stop=(di == 0),
                )
                if di == 1:
                    nc.tensor.matmul(
                        out=esh[:, kk, 1:8:2, :],
                        lhsT=wide[:, kk, 256 - sh : 384 - sh],
                        rhs=e0[:, 0:8:2, :],
                        start=False,
                        stop=True,
                    )
                if di == -1:
                    nc.tensor.matmul(
                        out=esh[:, kk, 0:8:2, :],
                        lhsT=wide[:, kk, -sh : 128 - sh],
                        rhs=e0[:, 1:8:2, :],
                        start=False,
                        stop=True,
                    )
            return esh

        def mask_classes(ks, shifted):
            n = len(range(ks.start, ks.stop, ks.step))
            nc.vector.tensor_tensor(
                out=prod[:, ks, :, :],
                in0=shifted,
                in1=m0.unsqueeze(1).to_broadcast([P, n, 8, NCLS]),
                op=ALU.mult,
            )

        def sum_classes(ks):
            nc.vector.tensor_reduce(out=sels[:, ks, :], in_=prod[:, ks, :, :], axis=AX.X, op=ALU.add)

        def nonzero():
            nc.vector.tensor_single_scalar(out=nz[:], in_=sels[:], scalar=0.0, op=ALU.not_equal)

        def count_taps():
            cp = psum.tile([P, 8], F32, name="cp", tag="tp", bufs=8 - ACC_BANKS)
            steps = []
            for k in range(TAPS):
                sh = shift[k]
                steps.append((cp[:], 128 + sh, nz[:, k, :]))
                if k >= 6:
                    steps.append((cp[:, 0:8:2], sh, nz[:, k, 1:8:2]))
                if k < 3:
                    steps.append((cp[:, 1:8:2], 256 + sh, nz[:, k, 0:8:2]))
            for i, (o, c0, r) in enumerate(steps):
                nc.tensor.matmul(
                    out=o, lhsT=wide[:, 1, c0 : c0 + P], rhs=r, start=(i == 0), stop=(i == len(steps) - 1)
                )
            nc.scalar.copy(out=cnt[:], in_=cp[:])

        def scale_count():
            nc.vector.tensor_scalar(
                out=ninth[:], in0=cnt[:], scalar1=1.0, scalar2=1.0 / 9.0, op0=ALU.max, op1=ALU.mult
            )

        def make_norm():
            nc.vector.reciprocal(out=norm[:], in_=ninth[:])

        wq = const.tile([P, TAPS, DIM], U32, name="wq", align_bytes=64)
        ws = const.tile([P, TAPS, DIM], U8, name="ws", align_bytes=64)
        wg = [const.tile([P, DIM, 4], BF16, name="wg%d" % k, align_bytes=64) for k in range(TAPS)]

        def regroup_w(copy, k, part, end):
            n = DIM // WPARTS
            copy(
                out=wg[k][:, part * n : end * n, :].rearrange("p (c i) t -> p c t i", i=4),
                in_=wraw[k][:, :, part * n : end * n].rearrange("p t (c i) -> p c t i", i=4),
            )

        def quantise_w(k):
            nc.vector.quantize_mx(
                out=wq[:, k, :].bitcast(FP8X4), scales=ws[:, k, :], in_=wg[k][:].rearrange("p d t -> p (d t)")
            )

        gts = {}
        psts = {}
        xq = {}
        xsc = {}
        acc = {}

        def gate(b, k):
            for mm in range(2):
                m = 2 * b + mm
                gt = gpool.tile([P, CH], BF16, name="gt", tag="gt")
                nc.vector.tensor_scalar_mul(
                    out=gt[:].rearrange("p (u w e) -> p u w e", u=2, e=2),
                    in0=xs[b][:, mm, :].rearrange("p (w u e) -> p u w e", u=2, e=2),
                    scalar1=sels[:, k, m : m + 1],
                )
                gts[(b, k, mm)] = gt

        def transpose(b, k, tag="tp"):
            pst = psum.tile([P, 2, PIX], F32, name="pst", tag=tag, bufs=ACC_BANKS if tag == "acc" else 8 - ACC_BANKS)
            for mm in range(2):
                words = gts[(b, k, mm)][:].bitcast(F32)
                for u in range(2):
                    nc.tensor.transpose(
                        out=pst[:, u, mm * P : (mm + 1) * P], in_=words[:, u * P : (u + 1) * P], identity=ident[:]
                    )
            psts[(b, k)] = pst

        def evacuate(b, k):
            sh = shift[k]
            d0, d1 = max(0, -sh), min(PIX, PIX - sh)
            nc.scalar.copy(
                out=gq[k][:, b % 3, 4 * d0 : 4 * d1].bitcast(F32).rearrange("p (x u) -> p x u", u=2),
                in_=psts[(b, k)][:, :, d0 + sh : d1 + sh].rearrange("p u x -> p x u"),
            )

        def quantise_x(b, k):
            q = xqpool.tile([P, PIX], U32, name="xq", tag="xq", align_bytes=64)
            s = xqpool.tile([P, PIX], U8, name="xsc", tag="xsc", align_bytes=64)
            nc.vector.quantize_mx(out=q[:].bitcast(FP8X4), scales=s[:], in_=gq[k][:, b % 3, :])
            xq[(b, k)], xsc[(b, k)] = q, s

        def multiply(b, k, mms=(0, 1)):
            for mm in mms:
                if k == ORDER[0]:
                    acc[(b, mm)] = psum.tile([P, DIM], F32, name="acc", tag="acc", bufs=ACC_BANKS)
                nc.tensor.matmul_mx(
                    out=acc[(b, mm)][:],
                    lhsT=xq[(b, k)][:, mm * P : (mm + 1) * P].bitcast(FP8X4),
                    lhsT_scale=xsc[(b, k)][:, mm * P : (mm + 1) * P],
                    rhs=wq[:, k, :].bitcast(FP8X4),
                    rhs_scale=ws[:, k, :],
                    start=(k == ORDER[0]),
                    stop=(k == ORDER[-1]),
                )

        def finish(b, mm, on_vector):
            m = 2 * b + mm
            res = rpool.tile([P, DIM], F32, name="res", tag="res")
            if on_vector:
                nc.vector.tensor_scalar_mul(out=res[:], in0=acc[(b, mm)][:], scalar1=norm[:, m : m + 1])
            else:
                nc.scalar.activation(out=res[:], in_=acc[(b, mm)][:], func=ACTF.Copy, scale=norm[:, m : m + 1])
            nc.sync.dma_start(out=ov[m * P : (m + 1) * P, :], in_=res[:])

        esh = {}
        for tg in (1, 0, 2):
            esh[tg] = shift_onehot(tg)
        sparts = [(k, part) for k in ORDER for part in range(WPARTS - v_parts[k])]

        def fill(n):
            for f in range(min(n, len(sparts))):
                k, part = sparts[0]
                regroup_w(nc.scalar.copy, k, part, part + 1)
                sparts.remove(sparts[0])


        def front(units):
            for b, k in units:
                gate(b, k)

        def middle(units, tag="tp"):
            for b, k in units:
                transpose(b, k, tag)
            for b, k in units:
                evacuate(b, k)

        def back(units):
            for b, k in units:
                quantise_x(b, k)

        def due(k):
            return min(i for i, c in enumerate(chunks) if k in [u[1] for u in c])

        def regroup_on_vector(j):
            for k in first_taps[j] if j < len(chunks) else []:
                if v_parts[k] > 0:
                    regroup_w(nc.vector.tensor_copy, k, WPARTS - v_parts[k], WPARTS)

        first_taps = [[k for k in ORDER if due(k) == j] for j in range(len(chunks))]
        rows = (slice(0, 3, 1), slice(3, 6, 2), slice(6, 9, 1))
        for ms in halves:
            nc.vector.tensor_tensor(out=prod[:, 4, ms, :], in0=e0[:, ms, :], in1=m0[:, ms, :], op=ALU.mult)
        for ms in halves:
            nc.vector.tensor_reduce(out=sels[:, 4, ms], in_=prod[:, 4, ms, :], axis=AX.X, op=ALU.add)
        mask_classes(rows[1], esh[1][:, 0:3:2, :, :])
        gate(0, ORDER[0])
        sum_classes(rows[1])
        regroup_on_vector(0)
        gate(1, ORDER[0])
        fill(HEAD_PARTS)
        for j in range(1, GLAG):
            front(chunks[j])
        for j in range(TLAG):
            middle(chunks[j])
        nc.scalar.copy(out=eshs[:], in_=esh[2][:])
        last = [(3, k) for k in ORDER]
        turns = chunks + [[(2, ORDER[-1]), last[0]], last[1:3], last[3:5]]
        for j in range(len(chunks)):
            middle(turns[j + TLAG])
            fill(max([-(-len([p for p in sparts if due(p[0]) - 1 <= j + i]) // i) for i in range(1, 12)]))
            for k in first_taps[j]:
                quantise_w(k)
            back(chunks[j])
            if j == 0:
                regroup_on_vector(1)
            if j == DOT0:
                mask_classes(rows[0], esh[0][:])
            if j == DOT2:
                mask_classes(rows[2], eshs[:])
            if j == COUNT + 2:
                scale_count()
            front(turns[j + GLAG][0:1])
            if j == DOT0:
                sum_classes(rows[0])
            if j == DOT2:
                sum_classes(rows[2])
            if j == COUNT + 2:
                make_norm()
            if j > 0:
                regroup_on_vector(j + 1)
            front(turns[j + GLAG][1:2])
            if j == DOT2:
                nonzero()
            for b, k in chunks[j]:
                multiply(b, k)
            if j == COUNT:
                count_taps()
        for mm in range(2):
            finish(0, mm, False)
        middle(turns[15])
        for mm in range(2):
            finish(1, mm, False)
        back(turns[13])
        front(last[5:9])
        back(turns[14])
        for b, k in turns[13] + turns[14]:
            multiply(b, k)
        back(turns[15])
        for mm in range(2):
            finish(2, mm, True)
        middle(last[5:9], "acc")
        back(last[5:9])
        for b, k in last[3:5]:
            multiply(b, k)
        for mm in range(2):
            for b, k in last[5:9]:
                multiply(b, k, (mm,))
            if mm == 0:
                finish(3, 0, False)
        for h in range(2):
            half = slice(h * (DIM // 2), (h + 1) * (DIM // 2))
            res = rpool.tile([P, DIM // 2], F32, name="half", tag="half")
            nc.scalar.activation(out=res[:], in_=acc[(3, 1)][:, half], func=ACTF.Copy, scale=norm[:, 7:8])
            nc.sync.dma_start(out=ov[7 * P : 8 * P, half], in_=res[:])
